import numpy as np
import ml_dtypes


def mxq(x, axis, fmt="e4m3"):
    dtype, down = {"e4m3": (ml_dtypes.float8_e4m3fn, 7), "e5m2": (ml_dtypes.float8_e5m2, 14)}[fmt]
    v = np.moveaxis(np.asarray(x, np.float32).astype(ml_dtypes.bfloat16).astype(np.float64), axis, -1)
    blocks = v.reshape(v.shape[:-1] + (-1, 32))
    amax = np.abs(blocks).max(-1, keepdims=True)
    byte = np.maximum(np.where(amax > 0, np.frexp(amax)[1] - 1 + 127, 0) - down, 1)
    scale = np.exp2(byte - 127.0)
    codes = (blocks / scale).astype(np.float32).astype(dtype).astype(np.float64)
    return np.moveaxis((codes * scale).reshape(v.shape), -1, axis)


WIDE = False


def mx_kscale(k):
    if not WIDE:
        return np.ones(k)
    levels = np.array([10, -10, 5, -5, 0])
    if k % 512:
        return np.exp2(np.random.permutation(np.resize(levels, k // 32))).repeat(32)
    a = np.empty((k // 512, 16))
    for p in range(k // 512):
        a[p, :8] = np.random.permutation(np.resize(levels, 8))
        for g in range(8):
            far = levels[np.abs(levels - a[p, g]) >= 10]
            a[p, g + 8] = far[np.random.randint(len(far))]
    return np.exp2(a.ravel()).repeat(32)


BF16 = ml_dtypes.bfloat16


def bf(x):
    return np.asarray(x, np.float32).astype(BF16)


def f64(x):
    return np.asarray(x).astype(np.float64)


E2M1 = np.array([0.0, 0.5, 1.0, 1.5, 2.0, 3.0, 4.0, 6.0, -0.0, -0.5, -1.0, -1.5, -2.0, -3.0, -4.0, -6.0])


def pack_weight(w, fmt):
    k, n = w.shape
    w = f64(bf(w)).reshape(k // 32, 32, n)
    amax = np.abs(w).max(1)
    if fmt == "e4m3":
        byte = np.frexp(amax)[1] - 1 + 127 - 7
    else:
        mant, ex = np.frexp(amax / 6.0)
        byte = np.where(mant > 0.5, ex, ex - 1) + 127
    byte = np.clip(np.where(amax > 0, byte, 1), 1, 254)
    scaled = (w * np.exp2(127.0 - byte)[:, None, :]).reshape(k, n).astype(np.float32)
    by_word = np.ascontiguousarray(scaled.reshape(k // 512, 128, 4, n).transpose(0, 1, 3, 2))
    if fmt == "e4m3":
        words = by_word.astype(ml_dtypes.float8_e4m3fn).view(np.uint8)
    else:
        c = by_word.astype(ml_dtypes.float4_e2m1fn).view(np.uint8) & 0xF
        words = c[..., 0::2] | (c[..., 1::2] << 4)
    return np.ascontiguousarray(words), np.ascontiguousarray(byte.astype(np.uint8).reshape(k // 512, 16, n))


def unpack_weight(words, scales, fmt):
    g, p, n, _ = words.shape
    if fmt == "e4m3":
        vals = np.ascontiguousarray(words).view(ml_dtypes.float8_e4m3fn).astype(np.float64)
    else:
        nib = np.empty((g, p, n, 4), np.uint8)
        nib[..., 0::2] = words & 0xF
        nib[..., 1::2] = words >> 4
        vals = E2M1[nib]
    vals = vals * np.repeat(np.exp2(scales.astype(np.float64) - 127.0), 8, axis=1)[..., None]
    return vals.transpose(0, 1, 3, 2).reshape(g * 512, n)
def pack4(w):
    words, scales = pack_weight(w, "e2m1")
    return words.reshape(words.shape[0], 128, -1), scales


def unpack4(words, scales):
    return unpack_weight(words.reshape(words.shape[0], 128, -1, 2), scales, "e2m1")


B, C, CI, N = 2, 1024, 512, 1024
EPS = 1e-5


def draw0():
    s, t = mx_kscale(N), mx_kscale(CI)
    r = np.random.standard_normal
    affinity = bf(r((B, N, N)) * 0.2 * s[None, None, :])
    g_x = bf(r((B, N, CI)) / s[None, :, None] * t[None, None, :])
    w_w = r((C, CI)) * 1.5 / (0.2 * np.sqrt(N) * np.sqrt(CI)) / t[None, :]
    words, scales = pack4(np.ascontiguousarray(w_w.T))
    return {"affinity": affinity,
            "g_x": g_x,
            "w_w_words": words,
            "w_w_scales": scales,
            "w_b": bf(r(C) * 0.3),
            "bn_gamma": bf(r(C)),
            "bn_beta": bf(r(C) * 0.5),
            "bn_mean": bf(r(C) * 0.5),
            "bn_var": bf(np.random.uniform(0.5, 1.5, C)),
            "x": bf(r((B, C, N)))}


def core(affinity, g_x, w_w_words, w_w_scales, w_b, bn_gamma, bn_beta, bn_mean, bn_var, x):
    y = (mxq(f64(affinity), 2, "e4m3") @ mxq(f64(g_x), 1, "e4m3")).transpose(0, 2, 1)
    wy = (unpack4(w_w_words, w_w_scales).T @ mxq(y, 1, "e4m3")) + f64(w_b)[None, :, None]
    inv_std = 1.0 / np.sqrt(f64(bn_var) + EPS)
    wy = f64(bn_gamma)[None, :, None] * (wy - f64(bn_mean)[None, :, None]) * inv_std[None, :, None] + f64(bn_beta)[None, :, None]
    return wy + f64(x)


def e4m3fn_bytes(y):
    return np.clip(np.asarray(y, np.float64), -448.0, 448.0).astype(np.float32).astype(ml_dtypes.float8_e4m3fn).view(np.uint8)


def e4m3fn_values(b):
    return np.asarray(b, np.uint8).view(ml_dtypes.float8_e4m3fn).astype(np.float64)


def setup_inputs():
    d = draw0()
    x0 = np.asarray(d['affinity']).astype(np.float64)
    s = (np.max(np.abs(x0), axis=(0, 1), keepdims=True) / 448.0).astype(np.float32)
    out = {}
    for k, v in d.items():
        if k == 'affinity':
            out['affinity_bytes'] = e4m3fn_bytes(x0 / s.astype(np.float64))
            out['affinity_scale'] = s
        else:
            out[k] = v
    return out


def reference(affinity_bytes, affinity_scale, g_x, w_w_words, w_w_scales, w_b, bn_gamma, bn_beta, bn_mean, bn_var, x):
    return core(e4m3fn_values(affinity_bytes) * affinity_scale.astype(np.float64), g_x, w_w_words, w_w_scales, w_b, bn_gamma, bn_beta, bn_mean, bn_var, x)

@@ -1,0 +1,370 @@
+from contextlib import ExitStack
+
+import concourse.mybir as mybir
+from concourse.masks import make_identity
+
+BATCH, C, CI, N = 2, 1024, 512, 1024
+EPS = 1e-5
+
+FLOPS = 2 * BATCH * (N * N * CI + C * CI * N)
+
+F32 = mybir.dt.float32
+BF16 = mybir.dt.bfloat16
+I32 = mybir.dt.int32
+U32 = mybir.dt.uint32
+U8 = mybir.dt.uint8
+FP8 = mybir.dt.float8_e4m3fn
+FP8X4 = mybir.dt.float8_e4m3fn_x4
+FP4X4 = mybir.dt.float4_e2m1fn_x4
+MULT = mybir.AluOpType.mult
+ADD = mybir.AluOpType.add
+SUB = mybir.AluOpType.subtract
+ACT = mybir.ActivationFunctionType
+
+P = 128
+PACK = 4
+K_PASS = P * PACK
+S_PASSES = N // K_PASS
+BLOCKS = N // P
+C_BLOCKS = C // P
+STEPS = BATCH * BLOCKS
+UNITS = ((0, 4), (4, 4), (8, 4), (12, 2), (14, 2))
+HALF = 4 * P
+
+
+def tile_sgcam_pb_w4_kernel(tc, affinity_bytes, affinity_scale, g_x, w_w_words, w_w_scales, w_b, bn_gamma, bn_beta, bn_mean, bn_var, x, out):
+    nc = tc.nc
+    with ExitStack() as ctx:
+        keep = ctx.enter_context(tc.tile_pool(name="keep", bufs=1))
+        work = ctx.enter_context(tc.tile_pool(name="work", bufs=4))
+        tp_pool = ctx.enter_context(tc.psum_pool(name="tp_pool", bufs=2))
+        y_pool = ctx.enter_context(tc.psum_pool(name="y_pool", bufs=2))
+        o_pool = ctx.enter_context(tc.psum_pool(name="o_pool", bufs=4))
+        ctx.enter_context(tc.manual_schedule())
+
+        ident = keep.tile([P, P], F32)
+        make_identity(nc, ident[:])
+        vec_rows = keep.tile([P, P], BF16)
+        nc.vector.memset(vec_rows[:], 0.0)
+        w_scales = keep.tile([P, C], U8, align_bytes=64)
+        nc.vector.memset(w_scales[:].bitcast(I32), 0)
+        one = keep.tile([P, 1], F32)
+        nc.vector.memset(one[:], 1.0)
+        warm = keep.tile([P, 1], F32)
+
+        k_scale = keep.tile([P, S_PASSES * PACK], F32)
+        nc.scalar.dma_start(out=k_scale[:].rearrange("p (g t) -> p g t", t=PACK), in_=affinity_scale.rearrange("a b (g p t) -> p (a b g) t", p=P, t=PACK))
+        nc.scalar.activation(out=warm[:], in_=one[:], func=ACT.Sqrt)
+
+        bytes_of = {}
+
+        def load_bytes(b, first, count):
+            codes_in = keep.tile([P, count, N], U8, name="codes_in_%d_%d" % (b, first))
+            nc.sync.dma_start(out=codes_in[:], in_=affinity_bytes[b, first * P : (first + count) * P, :].rearrange("(i p) k -> p i k", p=P))
+            for i in range(count):
+                bytes_of[b * BLOCKS + first + i] = codes_in[:, i, :]
+
+        g_raw = {}
+
+        def load_g(b, g):
+            raw = keep.tile([P, PACK, CI], BF16, name="g_raw_%d_%d" % (b, g))
+            nc.sync.dma_start(out=raw[:], in_=g_x[b, g * K_PASS : (g + 1) * K_PASS, :].rearrange("(p j) n -> p j n", j=PACK))
+            g_raw[b, g] = raw
+
+        x_raw = {}
+
+        def load_x(b, j):
+            raw = keep.tile([P, 2, N], BF16, name="x_raw_%d_%d" % (b, j))
+            nc.sync.dma_start(out=raw[:], in_=x[b, j * P : (j + 2) * P, :].rearrange("(i p) n -> p i n", p=P))
+            x_raw[b, j] = raw[:, 0, :]
+            x_raw[b, j + 1] = raw[:, 1, :]
+
+        load_bytes(0, 0, 1)
+        load_g(0, 0)
+        load_bytes(0, 1, 1)
+        load_g(0, 1)
+        load_bytes(0, 2, 2)
+        load_bytes(0, 4, 4)
+        for v, row in enumerate((w_b, bn_gamma, bn_beta, bn_mean, bn_var)):
+            nc.sync.dma_start(out=vec_rows[v * C_BLOCKS : (v + 1) * C_BLOCKS, :], in_=row.rearrange("(j p) -> j p", p=P))
+        w_codes = keep.tile([P, 2 * C], U8, align_bytes=64)
+        nc.sync.dma_start(out=w_codes[:], in_=w_w_words[0])
+        for q in range(4):
+            nc.sync.dma_start(out=w_scales[32 * q : 32 * q + 4, :].bitcast(I32), in_=w_w_scales[0, 4 * q : 4 * q + 4, :].bitcast(I32))
+        load_x(0, 0)
+        load_x(0, 2)
+        load_bytes(1, 0, 4)
+        load_x(0, 4)
+        load_g(1, 0)
+        load_x(0, 6)
+        load_g(1, 1)
+        load_bytes(1, 4, 4)
+        for j in range(0, C_BLOCKS, 2):
+            load_x(1, j)
+
+        wide = {}
+        grouped = {}
+        a_codes = {}
+        a_scales = {}
+        g_grouped = {}
+        g_codes = {}
+        g_scales = {}
+        tp = {}
+        y_ps = {}
+        y_bf = {}
+        y_codes = {}
+        y_scales = {}
+        o_ps = {}
+        vec = {}
+        x_plus = {}
+
+        def widen(s):
+            w = work.tile([P, N], BF16, name="w")
+            nc.scalar.copy(out=w[:], in_=bytes_of[s].bitcast(FP8))
+            wide[s] = w
+
+        def turn(s):
+            t = tp_pool.tile([P, 2 * S_PASSES * P], F32, name="t")
+            words = wide[s][:].bitcast(F32)
+            for u in range(2):
+                for g in range(S_PASSES):
+                    i = u * S_PASSES + g
+                    nc.tensor.transpose(t[:, i * P : (i + 1) * P], words[:, 256 * g + u : 256 * (g + 1) : 2], ident[:])
+            tp[s] = t
+
+        def scale(s):
+            gr = work.tile([P, S_PASSES * P * PACK], BF16, name="gr", align_bytes=64)
+            shape = [P, S_PASSES, P, 2, 2]
+            nc.vector.tensor_tensor(
+                out=gr[:].rearrange("p (g q u e) -> p g q u e", g=S_PASSES, u=2, e=2),
+                in0=tp[s][:].bitcast(BF16).rearrange("p (u g q e) -> p g q u e", u=2, g=S_PASSES, e=2),
+                in1=k_scale[:].rearrange("p (g o u e) -> p g o u e", g=S_PASSES, o=1, u=2, e=2).to_broadcast(shape),
+                op=MULT,
+            )
+            grouped[s] = gr
+
+        def quantize_a(s):
+            ac = work.tile([P, S_PASSES * P], U32, name="ac", align_bytes=64)
+            asc = work.tile([P, S_PASSES * P], U8, name="asc", align_bytes=64)
+            nc.vector.quantize_mx(out=ac[:].bitcast(FP8X4), scales=asc[:], in_=grouped[s][:])
+            a_codes[s] = ac
+            a_scales[s] = asc
+
+        def group_g(b, g, engine):
+            gg = keep.tile([P, PACK * CI], BF16, name="gg_%d_%d" % (b, g), align_bytes=64)
+            src = g_raw[b, g][:].rearrange("p j (m t) -> p t m j", t=PACK)
+            dst = gg[:].rearrange("p (t m j) -> p t m j", t=PACK, j=PACK)
+            if engine == "vector":
+                nc.vector.tensor_copy(out=dst, in_=src)
+            elif engine == "scalar":
+                nc.scalar.copy(out=dst, in_=src)
+            else:
+                for t in range(PACK):
+                    nc.gpsimd.tensor_scalar(out=dst[:, t], in0=src[:, t], scalar1=1.0, scalar2=0.0, op0=MULT, op1=ADD)
+            g_grouped[b, g] = gg
+
+        def quantize_g(b, g):
+            gc = keep.tile([P, CI], U32, name="gc_%d_%d" % (b, g), align_bytes=64)
+            gs = keep.tile([P, CI], U8, name="gs_%d_%d" % (b, g), align_bytes=64)
+            nc.vector.quantize_mx(out=gc[:].bitcast(FP8X4), scales=gs[:], in_=g_grouped[b, g][:])
+            g_codes[b, g] = gc
+            g_scales[b, g] = gs
+
+        def aggregate(s):
+            b = s // BLOCKS
+            y = y_pool.tile([P, PACK, P], F32, name="y")
+            for t in range(PACK):
+                for g in range(S_PASSES):
+                    nc.tensor.matmul_mx(
+                        out=y[:, t, :],
+                        lhsT=g_codes[b, g][:, t * P : (t + 1) * P].bitcast(FP8X4),
+                        lhsT_scale=g_scales[b, g][:, t * P : (t + 1) * P],
+                        rhs=a_codes[s][:, g * P : (g + 1) * P].bitcast(FP8X4),
+                        rhs_scale=a_scales[s][:, g * P : (g + 1) * P],
+                        start=(g == 0),
+                        stop=(g == S_PASSES - 1),
+                    )
+            y_ps[s] = y
+
+        def interleave_y(s):
+            yb = work.tile([P, P, PACK], BF16, name="yb", align_bytes=64)
+            nc.scalar.copy(out=yb[:], in_=y_ps[s][:].rearrange("p t q -> p q t"))
+            y_bf[s] = yb
+
+        def quantize_y(s):
+            unit = max(n for n in range(len(UNITS)) if UNITS[n][0] <= s)
+            i = s - UNITS[unit][0]
+            if i == 0:
+                yc = work.tile([P, HALF], U32, name="yc", align_bytes=64)
+                ys = work.tile([P, HALF], U8, name="ys", align_bytes=64)
+                y_codes[unit] = yc
+                y_scales[unit] = ys
+            cols = slice(i * P, (i + 1) * P)
+            nc.vector.quantize_mx(out=y_codes[unit][:, cols].bitcast(FP8X4), scales=y_scales[unit][:, cols], in_=y_bf[s][:].rearrange("p q t -> p (q t)"))
+
+        def project(unit, j):
+            width = UNITS[unit][1] * P
+            o = o_pool.tile([P, HALF], F32, name="o")
+            nc.tensor.matmul_mx(
+                out=o[:, 0:width],
+                lhsT=w_codes[:, j * 2 * P : (j + 1) * 2 * P].bitcast(FP4X4),
+                lhsT_scale=w_scales[:, j * P : (j + 1) * P],
+                rhs=y_codes[unit][:, 0:width].bitcast(FP8X4),
+                rhs_scale=y_scales[unit][:, 0:width],
+                start=True,
+                stop=True,
+            )
+            o_ps[unit, j] = o[:, 0:width]
+
+        def place(unit):
+            first, count = UNITS[unit]
+            b, i = divmod(first, BLOCKS)
+            return b, count * P, slice(i * P, (i + count) * P)
+
+        def store(unit, j, res):
+            b, width, cols = place(unit)
+            nc.sync.dma_start(out=out[b, j * P : (j + 1) * P, cols], in_=res)
+
+        def finish_vector(unit, j):
+            b, width, cols = place(unit)
+            rv = work.tile([P, HALF], F32, name="rv", bufs=6)
+            nc.vector.scalar_tensor_tensor(out=rv[:, 0:width], in0=o_ps[unit, j], scalar=vec["a"][:, j : j + 1], in1=x_plus[b, j][:, cols], op0=MULT, op1=ADD)
+            store(unit, j, rv[:, 0:width])
+
+        half_done = {}
+
+        def finish_scalar(unit, j):
+            width = place(unit)[1]
+            hd = work.tile([P, HALF], F32, name="hd")
+            nc.scalar.activation(out=hd[:, 0:width], in_=o_ps[unit, j], func=ACT.Identity, bias=vec["d"][:, j : j + 1], scale=vec["a"][:, j : j + 1])
+            half_done[unit, j] = hd[:, 0:width]
+
+        def finish_gpsimd(unit, j):
+            b, width, cols = place(unit)
+            rs = work.tile([P, HALF], F32, name="rs")
+            nc.gpsimd.tensor_tensor(out=rs[:, 0:width], in0=half_done[unit, j], in1=x_raw[b, j][:, cols], op=ADD)
+            store(unit, j, rs[:, 0:width])
+
+        def add_shift(b, j, cols):
+            if (b, j) not in x_plus:
+                x_plus[b, j] = keep.tile([P, N], F32, name="x_plus_%d_%d" % (b, j))
+            if (b, j) in XS:
+                nc.scalar.activation(out=x_plus[b, j][:, cols], in_=x_raw[b, j][:, cols], func=ACT.Identity, bias=vec["d"][:, j : j + 1])
+            else:
+                nc.gpsimd.tensor_scalar(out=x_plus[b, j][:, cols], in0=x_raw[b, j][:, cols], scalar1=1.0, scalar2=vec["d"][:, j : j + 1], op0=MULT, op1=ADD)
+
+        cols5 = keep.tile([P, 5, C_BLOCKS], F32)
+        var_eps = keep.tile([P, C_BLOCKS], F32)
+        std = keep.tile([P, C_BLOCKS], F32)
+        vec_f32 = keep.tile([P, P], F32)
+
+        def vec_turn():
+            nc.gpsimd.tensor_copy(out=vec_f32[:], in_=vec_rows[:])
+            vec_ps = o_pool.tile([P, HALF], F32, name="o")
+            nc.tensor.transpose(vec_ps[:, 0:P], vec_f32[:], ident[:])
+            vec["ps"] = vec_ps
+
+        def vec_copy():
+            nc.scalar.copy(out=cols5[:].rearrange("p v j -> p (v j)"), in_=vec["ps"][:, 0 : 5 * C_BLOCKS])
+            nc.gpsimd.tensor_scalar(out=var_eps[:], in0=cols5[:, 4, :], scalar1=1.0, scalar2=EPS, op0=MULT, op1=ADD)
+
+        def vec_sqrt():
+            nc.scalar.activation(out=std[:], in_=var_eps[:], func=ACT.Sqrt)
+
+        def fold_norm():
+            rstd = keep.tile([P, C_BLOCKS], F32, name="rstd")
+            nc.vector.reciprocal(out=rstd[:], in_=std[:])
+            a = keep.tile([P, C_BLOCKS], F32, name="a")
+            nc.gpsimd.tensor_tensor(out=a[:], in0=cols5[:, 1, :], in1=rstd[:], op=MULT)
+            shift = keep.tile([P, C_BLOCKS], F32, name="shift")
+            nc.gpsimd.tensor_tensor(out=shift[:], in0=cols5[:, 0, :], in1=cols5[:, 3, :], op=SUB)
+            scaled = keep.tile([P, C_BLOCKS], F32, name="scaled")
+            nc.gpsimd.tensor_tensor(out=scaled[:], in0=shift[:], in1=a[:], op=MULT)
+            d = keep.tile([P, C_BLOCKS], F32, name="d")
+            nc.gpsimd.tensor_tensor(out=d[:], in0=scaled[:], in1=cols5[:, 2, :], op=ADD)
+            vec["a"] = a
+            vec["d"] = d
+
+        XS = ()
+        EPI = {}
+        EPI.setdefault(6, []).append((0, [0], [1]))
+        EPI.setdefault(7, []).append((0, [2], [3]))
+        EPI.setdefault(8, []).append((0, [4], [5]))
+        EPI.setdefault(9, []).append((0, [6], [7]))
+        EPI.setdefault(10, []).append((1, [0], [1]))
+        EPI.setdefault(11, []).append((1, [2], [3]))
+        EPI.setdefault(12, []).append((1, [4], [5]))
+        EPI.setdefault(13, []).append((1, [6], [7]))
+        EPI.setdefault(14, []).append((2, [0], [1]))
+        EPI.setdefault(14, []).append((2, [2], [3]))
+        EPI.setdefault(15, []).append((2, [4], [5]))
+        EPI.setdefault(16, []).append((2, [6], [7]))
+        EPI.setdefault(16, []).append((3, [0], [1]))
+        EPI.setdefault(17, []).append((3, [2], [3]))
+        EPI.setdefault(17, []).append((3, [4], [5]))
+        EPI.setdefault(17, []).append((3, [6], [7]))
+        EPI.setdefault(18, []).append((4, [0], [1]))
+        EPI.setdefault(18, []).append((4, [2], [3]))
+        EPI.setdefault(18, []).append((4, [4], [5]))
+        EPI.setdefault(18, []).append((4, [6], [7]))
+        AGG = {1: [], 2: [0, 1]}
+        FQ = {2: [], 3: [0, 1], 16: [14, 15]}
+        PLUS = {5: [(0, 0)], 6: [(0, 2)], 7: [(0, 4)], 8: [(0, 6)], 10: [(1, 0)], 11: [(1, 2)], 12: [(1, 4)], 13: [(1, 6)]}
+        LEAD = 3
+        for s in range(LEAD):
+            widen(s)
+        turn(0)
+        group_g(0, 0, "vector")
+        group_g(0, 1, "gpsimd")
+        for s in range(STEPS + 4):
+            ready = AGG.get(s, [s - 1] if 1 <= s <= STEPS else [])
+            if s == 0:
+                turn(1)
+                turn(2)
+            for i in ready:
+                aggregate(i)
+            if s == 1:
+                vec_turn()
+            if 1 <= s and s + 2 < STEPS and 1 == 2:
+                turn(s + 2)
+            if 2 <= s and s + 1 < STEPS and 1 == 1:
+                turn(s + 1)
+            for unit, vs, ss in EPI.get(s, []):
+                for j in ss:
+                    finish_scalar(unit, j)
+            if s + LEAD < STEPS:
+                widen(s + LEAD)
+            for i in ready:
+                interleave_y(i)
+            if s == 2:
+                vec_copy()
+            if s == 3:
+                vec_sqrt()
+            if s < STEPS:
+                scale(s)
+            if s < 2:
+                quantize_g(0, s)
+            fq = FQ.get(s, [s - 2] if 3 <= s < STEPS else [])
+            for unit, vs, ss in EPI.get(s, []):
+                for j in vs:
+                    finish_vector(unit, j)
+            for i in fq:
+                quantize_y(i)
+            if s < STEPS:
+                quantize_a(s)
+            for unit, vs, ss in EPI.get(s + 1, []):
+                for j in vs + ss:
+                    project(unit, j)
+            if s == 3:
+                fold_norm()
+            for unit, vs, ss in EPI.get(s, []):
+                for j in ss:
+                    finish_gpsimd(unit, j)
+            for b, j in PLUS.get(s, []):
+                add_shift(b, j, slice(0, N))
+            if s == 6:
+                group_g(1, 0, "scalar")
+            if s == 5:
+                group_g(1, 1, "gpsimd")
+            if s in (7, 8):
+                quantize_g(1, s - 7)

@@ -52,10 +52,6 @@ def tile_sgcam_pb_w4_kernel(tc, affinity_bytes, affinity_scale, g_x, w_w_words, 
         nc.vector.memset(one[:], 1.0)
         warm = keep.tile([P, 1], F32)
 
-        k_scale = keep.tile([P, S_PASSES * PACK], F32)
-        nc.scalar.dma_start(out=k_scale[:].rearrange("p (g t) -> p g t", t=PACK), in_=affinity_scale.rearrange("a b (g p t) -> p (a b g) t", p=P, t=PACK))
-        nc.scalar.activation(out=warm[:], in_=one[:], func=ACT.Sqrt)
-
         bytes_of = {}
 
         def load_bytes(b, first, count):
@@ -79,6 +75,9 @@ def tile_sgcam_pb_w4_kernel(tc, affinity_bytes, affinity_scale, g_x, w_w_words, 
             x_raw[b, j] = raw[:, 0, :]
             x_raw[b, j + 1] = raw[:, 1, :]
 
+        k_scale = keep.tile([P, S_PASSES * PACK], F32)
+        nc.scalar.dma_start(out=k_scale[:].rearrange("p (g t) -> p g t", t=PACK), in_=affinity_scale.rearrange("a b (g p t) -> p (a b g) t", p=P, t=PACK))
+        nc.scalar.activation(out=warm[:], in_=one[:], func=ACT.Sqrt)
         load_bytes(0, 0, 1)
         load_g(0, 0)
         load_bytes(0, 1, 1)
@@ -87,6 +86,7 @@ def tile_sgcam_pb_w4_kernel(tc, affinity_bytes, affinity_scale, g_x, w_w_words, 
         load_bytes(0, 4, 4)
         for v, row in enumerate((w_b, bn_gamma, bn_beta, bn_mean, bn_var)):
             nc.sync.dma_start(out=vec_rows[v * C_BLOCKS : (v + 1) * C_BLOCKS, :], in_=row.rearrange("(j p) -> j p", p=P))
+        load_g(1, 0)
         w_codes = keep.tile([P, 2 * C], U8, align_bytes=64)
         nc.sync.dma_start(out=w_codes[:], in_=w_w_words[0])
         for q in range(4):
@@ -94,10 +94,9 @@ def tile_sgcam_pb_w4_kernel(tc, affinity_bytes, affinity_scale, g_x, w_w_words, 
         load_x(0, 0)
         load_x(0, 2)
         load_bytes(1, 0, 4)
-        load_x(0, 4)
-        load_g(1, 0)
-        load_x(0, 6)
         load_g(1, 1)
+        load_x(0, 4)
+        load_x(0, 6)
         load_bytes(1, 4, 4)
         for j in range(0, C_BLOCKS, 2):
             load_x(1, j)
@@ -227,8 +226,8 @@ def tile_sgcam_pb_w4_kernel(tc, affinity_bytes, affinity_scale, g_x, w_w_words, 
 
         def finish_vector(unit, j):
             b, width, cols = place(unit)
-            rv = work.tile([P, HALF], F32, name="rv", bufs=6)
-            nc.vector.scalar_tensor_tensor(out=rv[:, 0:width], in0=o_ps[unit, j], scalar=vec["a"][:, j : j + 1], in1=x_plus[b, j][:, cols], op0=MULT, op1=ADD)
+            rv = work.tile([P, HALF], F32, name="rv", bufs=8)
+            nc.vector.scalar_tensor_tensor(out=rv[:, 0:width], in0=o_ps[unit, j], scalar=vec["a"][:, j : j + 1], in1=x_plus[unit, j], op0=MULT, op1=ADD)
             store(unit, j, rv[:, 0:width])
 
         half_done = {}
@@ -245,13 +244,27 @@ def tile_sgcam_pb_w4_kernel(tc, affinity_bytes, affinity_scale, g_x, w_w_words, 
             nc.gpsimd.tensor_tensor(out=rs[:, 0:width], in0=half_done[unit, j], in1=x_raw[b, j][:, cols], op=ADD)
             store(unit, j, rs[:, 0:width])
 
-        def add_shift(b, j, cols):
-            if (b, j) not in x_plus:
-                x_plus[b, j] = keep.tile([P, N], F32, name="x_plus_%d_%d" % (b, j))
-            if (b, j) in XS:
-                nc.scalar.activation(out=x_plus[b, j][:, cols], in_=x_raw[b, j][:, cols], func=ACT.Identity, bias=vec["d"][:, j : j + 1])
+        def add_shift(unit, j):
+            b, width, cols = place(unit)
+            xp = work.tile([P, HALF], F32, name="xp", bufs=6)
+            if j in (0, 4):
+                nc.gpsimd.tensor_scalar(out=xp[:, 0:width], in0=x_raw[b, j][:, cols], scalar1=1.0, scalar2=vec["d"][:, j : j + 1], op0=MULT, op1=ADD)
             else:
-                nc.gpsimd.tensor_scalar(out=x_plus[b, j][:, cols], in0=x_raw[b, j][:, cols], scalar1=1.0, scalar2=vec["d"][:, j : j + 1], op0=MULT, op1=ADD)
+                nc.scalar.activation(out=xp[:, 0:width], in_=x_raw[b, j][:, cols], func=ACT.Identity, bias=vec["d"][:, j : j + 1])
+            x_plus[unit, j] = xp[:, 0:width]
+
+        def group_piece(b, g, t, engine):
+            if t == 0:
+                gg = keep.tile([P, PACK * CI], BF16, name="gg_%d_%d" % (b, g), align_bytes=64)
+                g_grouped[b, g] = gg
+            src = g_raw[b, g][:].rearrange("p j (m t) -> p t m j", t=PACK)[:, t]
+            dst = g_grouped[b, g][:].rearrange("p (t m j) -> p t m j", t=PACK, j=PACK)[:, t]
+            if engine == "vector":
+                nc.vector.tensor_copy(out=dst, in_=src)
+            elif engine == "gpsimd":
+                nc.gpsimd.tensor_scalar(out=dst, in0=src, scalar1=1.0, scalar2=0.0, op0=MULT, op1=ADD)
+            else:
+                nc.scalar.copy(out=dst, in_=src)
 
         cols5 = keep.tile([P, 5, C_BLOCKS], F32)
         var_eps = keep.tile([P, C_BLOCKS], F32)
@@ -285,86 +298,82 @@ def tile_sgcam_pb_w4_kernel(tc, affinity_bytes, affinity_scale, g_x, w_w_words, 
             vec["a"] = a
             vec["d"] = d
 
-        XS = ()
         EPI = {}
         EPI.setdefault(6, []).append((0, [0], [1]))
         EPI.setdefault(7, []).append((0, [2], [3]))
         EPI.setdefault(8, []).append((0, [4], [5]))
-        EPI.setdefault(9, []).append((0, [6], [7]))
+        EPI.setdefault(9, []).append((0, [6,7], []))
         EPI.setdefault(10, []).append((1, [0], [1]))
         EPI.setdefault(11, []).append((1, [2], [3]))
         EPI.setdefault(12, []).append((1, [4], [5]))
-        EPI.setdefault(13, []).append((1, [6], [7]))
+        EPI.setdefault(13, []).append((1, [6,7], []))
         EPI.setdefault(14, []).append((2, [0], [1]))
-        EPI.setdefault(14, []).append((2, [2], [3]))
-        EPI.setdefault(15, []).append((2, [4], [5]))
-        EPI.setdefault(16, []).append((2, [6], [7]))
-        EPI.setdefault(16, []).append((3, [0], [1]))
-        EPI.setdefault(17, []).append((3, [2], [3]))
-        EPI.setdefault(17, []).append((3, [4], [5]))
-        EPI.setdefault(17, []).append((3, [6], [7]))
-        EPI.setdefault(18, []).append((4, [0], [1]))
-        EPI.setdefault(18, []).append((4, [2], [3]))
-        EPI.setdefault(18, []).append((4, [4], [5]))
-        EPI.setdefault(18, []).append((4, [6], [7]))
-        AGG = {1: [], 2: [0, 1]}
-        FQ = {2: [], 3: [0, 1], 16: [14, 15]}
-        PLUS = {5: [(0, 0)], 6: [(0, 2)], 7: [(0, 4)], 8: [(0, 6)], 10: [(1, 0)], 11: [(1, 2)], 12: [(1, 4)], 13: [(1, 6)]}
-        LEAD = 3
-        for s in range(LEAD):
+        EPI.setdefault(15, []).append((2, [2], [3]))
+        EPI.setdefault(16, []).append((2, [4], [5]))
+        EPI.setdefault(16, []).append((2, [6,7], []))
+        EPI.setdefault(17, []).append((3, [0,1], [3]))
+        EPI.setdefault(17, []).append((3, [2], []))
+        EPI.setdefault(17, []).append((3, [4,5], [7]))
+        EPI.setdefault(17, []).append((3, [6], []))
+        EPI.setdefault(18, []).append((4, [0,1], [3]))
+        EPI.setdefault(18, []).append((4, [2], []))
+        EPI.setdefault(18, []).append((4, [4,5], [7]))
+        EPI.setdefault(18, []).append((4, [6], []))
+        DG = {s: ((s - 1) // 4, (s - 1) % 4) for s in range(1, 9)}
+        for s in range(3):
             widen(s)
-        turn(0)
-        group_g(0, 0, "vector")
-        group_g(0, 1, "gpsimd")
-        for s in range(STEPS + 4):
-            ready = AGG.get(s, [s - 1] if 1 <= s <= STEPS else [])
             if s == 0:
-                turn(1)
-                turn(2)
-            for i in ready:
+                turn(0)
+        group_g(0, 0, "vector")
+        for t in range(4):
+            group_piece(0, 1, t, "scalar" if t < 2 else "vector")
+        turn(1)
+        for s in range(STEPS + 6):
+            n = s - 1
+            agg = {1: [], 2: [0, 1]}.get(s, [n] if 0 <= n < STEPS else [])
+            epi = EPI.get(s, [])
+            for i in agg:
                 aggregate(i)
             if s == 1:
                 vec_turn()
-            if 1 <= s and s + 2 < STEPS and 1 == 2:
+            if s + 2 < STEPS:
                 turn(s + 2)
-            if 2 <= s and s + 1 < STEPS and 1 == 1:
-                turn(s + 1)
-            for unit, vs, ss in EPI.get(s, []):
+            for unit, vs, ss in epi:
                 for j in ss:
                     finish_scalar(unit, j)
-            if s + LEAD < STEPS:
-                widen(s + LEAD)
-            for i in ready:
+            if s + 3 < STEPS:
+                widen(s + 3)
+            for i in agg:
                 interleave_y(i)
-            if s == 2:
+            if s == 1 + 1:
                 vec_copy()
-            if s == 3:
+            if s == 1 + 2:
                 vec_sqrt()
             if s < STEPS:
                 scale(s)
             if s < 2:
                 quantize_g(0, s)
-            fq = FQ.get(s, [s - 2] if 3 <= s < STEPS else [])
-            for unit, vs, ss in EPI.get(s, []):
-                for j in vs:
-                    finish_vector(unit, j)
-            for i in fq:
-                quantize_y(i)
+            half = len(epi) // 2 if len(epi) > 1 else 0
+            flat = [(unit, j) for unit, vs, ss in epi for j in vs]
+            for unit, j in flat[: (len(flat) + 1) // 2]:
+                finish_vector(unit, j)
+            for m in {2: [], 3: [0, 1], 16: [14, 15]}.get(s, [s - 2] if 3 <= s < STEPS else []):
+                quantize_y(m)
             if s < STEPS:
                 quantize_a(s)
+            for unit, j in flat[(len(flat) + 1) // 2 :]:
+                finish_vector(unit, j)
+            if s == 4:
+                fold_norm()
             for unit, vs, ss in EPI.get(s + 1, []):
+                for j in vs:
+                    add_shift(unit, j)
                 for j in vs + ss:
                     project(unit, j)
-            if s == 3:
-                fold_norm()
-            for unit, vs, ss in EPI.get(s, []):
+            if s in DG:
+                group_piece(1, DG[s][0], DG[s][1], "gpsimd")
+            if s in (7, 8):
+                quantize_g(1, (7, 8).index(s))
+            for unit, vs, ss in epi:
                 for j in ss:
                     finish_gpsimd(unit, j)
-            for b, j in PLUS.get(s, []):
-                add_shift(b, j, slice(0, N))
-            if s == 6:
-                group_g(1, 0, "scalar")
-            if s == 5:
-                group_g(1, 1, "gpsimd")
-            if s in (7, 8):
-                quantize_g(1, s - 7)

@@ -24,12 +24,27 @@ ACT = mybir.ActivationFunctionType
 P = 128
 PACK = 4
 K_PASS = P * PACK
-S_PASSES = N // K_PASS
-BLOCKS = N // P
+PASSES = N // K_PASS
+ROW_BLOCKS = N // P
+BLOCKS = BATCH * ROW_BLOCKS
 C_BLOCKS = C // P
-STEPS = BATCH * BLOCKS
+UNIT_COLS = 512
+FP4_BYTES = 2
+
 UNITS = ((0, 4), (4, 4), (8, 4), (12, 2), (14, 2))
-HALF = 4 * P
+HALF_UNITS = (3, 4)
+
+WIDEN_LEAD = 3
+TURN_LEAD = 2
+SHIFT_LEAD = 2
+Y_QUANTIZE_STEP = (5, 10, 13, 15, 17)
+FINISH_STEPS = ((7, 8, 9, 10), (11, 11, 12, 13), (15, 15, 16, 16), (17, 17, 17, 17), (18, 18, 19, 19))
+SCALAR_SIDE_FULL = (1, 3, 5, 7)
+SCALAR_SIDE_HALF = (3, 7)
+PAIRS_FULL = ((0, 1), (2, 3), (4, 5), (6, 7))
+PAIRS_HALF = ((0, 1, 3), (2,), (4, 5, 7), (6,))
+SHIFT_ON_GPSIMD = (0, 4)
+STEPS = FINISH_STEPS[-1][-1] + 1
 
 
 def tile_sgcam_pb_w4_kernel(tc, affinity_bytes, affinity_scale, g_x, w_w_words, w_w_scales, w_b, bn_gamma, bn_beta, bn_mean, bn_var, x, out):
@@ -37,9 +52,9 @@ def tile_sgcam_pb_w4_kernel(tc, affinity_bytes, affinity_scale, g_x, w_w_words, 
     with ExitStack() as ctx:
         keep = ctx.enter_context(tc.tile_pool(name="keep", bufs=1))
         work = ctx.enter_context(tc.tile_pool(name="work", bufs=4))
-        tp_pool = ctx.enter_context(tc.psum_pool(name="tp_pool", bufs=2))
+        turn_pool = ctx.enter_context(tc.psum_pool(name="turn_pool", bufs=2))
         y_pool = ctx.enter_context(tc.psum_pool(name="y_pool", bufs=2))
-        o_pool = ctx.enter_context(tc.psum_pool(name="o_pool", bufs=4))
+        out_pool = ctx.enter_context(tc.psum_pool(name="out_pool", bufs=4))
         ctx.enter_context(tc.manual_schedule())
 
         ident = keep.tile([P, P], F32)
@@ -50,72 +65,62 @@ def tile_sgcam_pb_w4_kernel(tc, affinity_bytes, affinity_scale, g_x, w_w_words, 
         nc.vector.memset(w_scales[:].bitcast(I32), 0)
         one = keep.tile([P, 1], F32)
         nc.vector.memset(one[:], 1.0)
-        warm = keep.tile([P, 1], F32)
+
+        k_scale = keep.tile([P, PASSES * PACK], F32)
+        nc.scalar.dma_start(out=k_scale[:].rearrange("p (g t) -> p g t", t=PACK), in_=affinity_scale.rearrange("a b (g p t) -> p (a b g) t", p=P, t=PACK))
+        root_of_one = keep.tile([P, 1], F32)
+        nc.scalar.activation(out=root_of_one[:], in_=one[:], func=ACT.Sqrt)
 
         bytes_of = {}
+        g_rows = {}
+        x_rows = {}
 
-        def load_bytes(b, first, count):
-            codes_in = keep.tile([P, count, N], U8, name="codes_in_%d_%d" % (b, first))
-            nc.sync.dma_start(out=codes_in[:], in_=affinity_bytes[b, first * P : (first + count) * P, :].rearrange("(i p) k -> p i k", p=P))
+        def load_bytes(first, count):
+            codes_in = keep.tile([P, count, N], U8, name="codes_in_%d" % first)
+            batch, row = divmod(first, ROW_BLOCKS)
+            nc.sync.dma_start(out=codes_in[:], in_=affinity_bytes[batch, row * P : (row + count) * P, :].rearrange("(i p) k -> p i k", p=P))
             for i in range(count):
-                bytes_of[b * BLOCKS + first + i] = codes_in[:, i, :]
+                bytes_of[first + i] = codes_in[:, i, :]
 
-        g_raw = {}
+        def load_g(batch, g):
+            rows = keep.tile([P, PACK, CI], BF16, name="g_rows_%d_%d" % (batch, g))
+            nc.sync.dma_start(out=rows[:], in_=g_x[batch, g * K_PASS : (g + 1) * K_PASS, :].rearrange("(p j) n -> p j n", j=PACK))
+            g_rows[batch, g] = rows
 
-        def load_g(b, g):
-            raw = keep.tile([P, PACK, CI], BF16, name="g_raw_%d_%d" % (b, g))
-            nc.sync.dma_start(out=raw[:], in_=g_x[b, g * K_PASS : (g + 1) * K_PASS, :].rearrange("(p j) n -> p j n", j=PACK))
-            g_raw[b, g] = raw
+        def load_x(batch, j):
+            rows = keep.tile([P, 2, N], BF16, name="x_rows_%d_%d" % (batch, j))
+            nc.sync.dma_start(out=rows[:], in_=x[batch, j * P : (j + 2) * P, :].rearrange("(i p) n -> p i n", p=P))
+            x_rows[batch, j] = rows[:, 0, :]
+            x_rows[batch, j + 1] = rows[:, 1, :]
 
-        x_raw = {}
-
-        def load_x(b, j):
-            raw = keep.tile([P, 2, N], BF16, name="x_raw_%d_%d" % (b, j))
-            nc.sync.dma_start(out=raw[:], in_=x[b, j * P : (j + 2) * P, :].rearrange("(i p) n -> p i n", p=P))
-            x_raw[b, j] = raw[:, 0, :]
-            x_raw[b, j + 1] = raw[:, 1, :]
-
-        k_scale = keep.tile([P, S_PASSES * PACK], F32)
-        nc.scalar.dma_start(out=k_scale[:].rearrange("p (g t) -> p g t", t=PACK), in_=affinity_scale.rearrange("a b (g p t) -> p (a b g) t", p=P, t=PACK))
-        nc.scalar.activation(out=warm[:], in_=one[:], func=ACT.Sqrt)
-        load_bytes(0, 0, 1)
+        load_bytes(0, 1)
         load_g(0, 0)
-        load_bytes(0, 1, 1)
+        load_bytes(1, 1)
         load_g(0, 1)
-        load_bytes(0, 2, 2)
-        load_bytes(0, 4, 4)
-        for v, row in enumerate((w_b, bn_gamma, bn_beta, bn_mean, bn_var)):
-            nc.sync.dma_start(out=vec_rows[v * C_BLOCKS : (v + 1) * C_BLOCKS, :], in_=row.rearrange("(j p) -> j p", p=P))
+        load_bytes(2, 2)
+        load_bytes(4, 4)
+        for v, vector in enumerate((w_b, bn_gamma, bn_beta, bn_mean, bn_var)):
+            nc.sync.dma_start(out=vec_rows[v * C_BLOCKS : (v + 1) * C_BLOCKS, :], in_=vector.rearrange("(j p) -> j p", p=P))
         load_g(1, 0)
-        w_codes = keep.tile([P, 2 * C], U8, align_bytes=64)
+        w_codes = keep.tile([P, FP4_BYTES * C], U8, align_bytes=64)
         nc.sync.dma_start(out=w_codes[:], in_=w_w_words[0])
         for q in range(4):
             nc.sync.dma_start(out=w_scales[32 * q : 32 * q + 4, :].bitcast(I32), in_=w_w_scales[0, 4 * q : 4 * q + 4, :].bitcast(I32))
         load_x(0, 0)
         load_x(0, 2)
-        load_bytes(1, 0, 4)
+        load_bytes(8, 4)
         load_g(1, 1)
         load_x(0, 4)
         load_x(0, 6)
-        load_bytes(1, 4, 4)
+        load_bytes(12, 4)
         for j in range(0, C_BLOCKS, 2):
             load_x(1, j)
 
         wide = {}
-        grouped = {}
+        turned = {}
+        scaled = {}
         a_codes = {}
         a_scales = {}
-        g_grouped = {}
-        g_codes = {}
-        g_scales = {}
-        tp = {}
-        y_ps = {}
-        y_bf = {}
-        y_codes = {}
-        y_scales = {}
-        o_ps = {}
-        vec = {}
-        x_plus = {}
 
         def widen(s):
             w = work.tile([P, N], BF16, name="w")
@@ -123,257 +128,250 @@ def tile_sgcam_pb_w4_kernel(tc, affinity_bytes, affinity_scale, g_x, w_w_words, 
             wide[s] = w
 
         def turn(s):
-            t = tp_pool.tile([P, 2 * S_PASSES * P], F32, name="t")
+            t = turn_pool.tile([P, 2 * PASSES * P], F32, name="t")
             words = wide[s][:].bitcast(F32)
             for u in range(2):
-                for g in range(S_PASSES):
-                    i = u * S_PASSES + g
+                for g in range(PASSES):
+                    i = u * PASSES + g
                     nc.tensor.transpose(t[:, i * P : (i + 1) * P], words[:, 256 * g + u : 256 * (g + 1) : 2], ident[:])
-            tp[s] = t
+            turned[s] = t
 
         def scale(s):
-            gr = work.tile([P, S_PASSES * P * PACK], BF16, name="gr", align_bytes=64)
-            shape = [P, S_PASSES, P, 2, 2]
+            pair, half = divmod(s, 2)
+            if half == 0:
+                sc = work.tile([P, 2 * N], BF16, name="sc", bufs=3, align_bytes=64)
+                scaled[pair] = sc
             nc.vector.tensor_tensor(
-                out=gr[:].rearrange("p (g q u e) -> p g q u e", g=S_PASSES, u=2, e=2),
-                in0=tp[s][:].bitcast(BF16).rearrange("p (u g q e) -> p g q u e", u=2, g=S_PASSES, e=2),
-                in1=k_scale[:].rearrange("p (g o u e) -> p g o u e", g=S_PASSES, o=1, u=2, e=2).to_broadcast(shape),
+                out=scaled[pair][:, half * N : (half + 1) * N].rearrange("p (g n u e) -> p g n u e", g=PASSES, u=2, e=2),
+                in0=turned[s][:].bitcast(BF16).rearrange("p (u g n e) -> p g n u e", u=2, g=PASSES, e=2),
+                in1=k_scale[:].rearrange("p (g o u e) -> p g o u e", g=PASSES, o=1, u=2, e=2).to_broadcast([P, PASSES, P, 2, 2]),
                 op=MULT,
             )
-            grouped[s] = gr
 
-        def quantize_a(s):
-            ac = work.tile([P, S_PASSES * P], U32, name="ac", align_bytes=64)
-            asc = work.tile([P, S_PASSES * P], U8, name="asc", align_bytes=64)
-            nc.vector.quantize_mx(out=ac[:].bitcast(FP8X4), scales=asc[:], in_=grouped[s][:])
-            a_codes[s] = ac
-            a_scales[s] = asc
+        def quantize_a(pair):
+            ac = work.tile([P, 2 * PASSES * P], U32, name="ac", bufs=3, align_bytes=64)
+            asc = work.tile([P, 2 * PASSES * P], U8, name="asc", bufs=3, align_bytes=64)
+            nc.vector.quantize_mx(out=ac[:].bitcast(FP8X4), scales=asc[:], in_=scaled[pair][:])
+            a_codes[pair] = ac
+            a_scales[pair] = asc
 
-        def group_g(b, g, engine):
-            gg = keep.tile([P, PACK * CI], BF16, name="gg_%d_%d" % (b, g), align_bytes=64)
-            src = g_raw[b, g][:].rearrange("p j (m t) -> p t m j", t=PACK)
-            dst = gg[:].rearrange("p (t m j) -> p t m j", t=PACK, j=PACK)
+        g_grouped = {}
+        g_codes = {}
+        g_scales = {}
+
+        def group_g(batch, g, first, last, engine):
+            if first == 0:
+                grouped = keep.tile([P, PACK * CI], BF16, name="g_grouped_%d_%d" % (batch, g), align_bytes=64)
+                g_grouped[batch, g] = grouped
+            src = g_rows[batch, g][:].rearrange("p j (m t) -> p t m j", t=PACK)[:, first:last]
+            dst = g_grouped[batch, g][:].rearrange("p (t m j) -> p t m j", t=PACK, j=PACK)[:, first:last]
             if engine == "vector":
                 nc.vector.tensor_copy(out=dst, in_=src)
             elif engine == "scalar":
                 nc.scalar.copy(out=dst, in_=src)
             else:
-                for t in range(PACK):
-                    nc.gpsimd.tensor_scalar(out=dst[:, t], in0=src[:, t], scalar1=1.0, scalar2=0.0, op0=MULT, op1=ADD)
-            g_grouped[b, g] = gg
+                nc.gpsimd.tensor_scalar(out=dst, in0=src, scalar1=1.0, scalar2=0.0, op0=MULT, op1=ADD)
 
-        def quantize_g(b, g):
-            gc = keep.tile([P, CI], U32, name="gc_%d_%d" % (b, g), align_bytes=64)
-            gs = keep.tile([P, CI], U8, name="gs_%d_%d" % (b, g), align_bytes=64)
-            nc.vector.quantize_mx(out=gc[:].bitcast(FP8X4), scales=gs[:], in_=g_grouped[b, g][:])
-            g_codes[b, g] = gc
-            g_scales[b, g] = gs
+        def quantize_g(batch, g):
+            gc = keep.tile([P, CI], U32, name="gc_%d_%d" % (batch, g), align_bytes=64)
+            gs = keep.tile([P, CI], U8, name="gs_%d_%d" % (batch, g), align_bytes=64)
+            nc.vector.quantize_mx(out=gc[:].bitcast(FP8X4), scales=gs[:], in_=g_grouped[batch, g][:])
+            g_codes[batch, g] = gc
+            g_scales[batch, g] = gs
+
+        y_banks = {}
+        y_rows = {}
+        y_codes = {}
+        y_scales = {}
+
+        def unit_of(s):
+            unit = max(n for n in range(len(UNITS)) if UNITS[n][0] <= s)
+            return unit, s - UNITS[unit][0]
 
         def aggregate(s):
-            b = s // BLOCKS
+            batch = s // ROW_BLOCKS
+            pair, half = divmod(s, 2)
             y = y_pool.tile([P, PACK, P], F32, name="y")
             for t in range(PACK):
-                for g in range(S_PASSES):
+                g_cols = slice(t * P, (t + 1) * P)
+                for g in range(PASSES):
+                    i = half * PASSES + g
+                    a_cols = slice(i * P, (i + 1) * P)
                     nc.tensor.matmul_mx(
                         out=y[:, t, :],
-                        lhsT=g_codes[b, g][:, t * P : (t + 1) * P].bitcast(FP8X4),
-                        lhsT_scale=g_scales[b, g][:, t * P : (t + 1) * P],
-                        rhs=a_codes[s][:, g * P : (g + 1) * P].bitcast(FP8X4),
-                        rhs_scale=a_scales[s][:, g * P : (g + 1) * P],
+                        lhsT=g_codes[batch, g][:, g_cols].bitcast(FP8X4),
+                        lhsT_scale=g_scales[batch, g][:, g_cols],
+                        rhs=a_codes[pair][:, a_cols].bitcast(FP8X4),
+                        rhs_scale=a_scales[pair][:, a_cols],
                         start=(g == 0),
-                        stop=(g == S_PASSES - 1),
+                        stop=(g == PASSES - 1),
                     )
-            y_ps[s] = y
+            y_banks[s] = y
 
         def interleave_y(s):
-            yb = work.tile([P, P, PACK], BF16, name="yb", align_bytes=64)
-            nc.scalar.copy(out=yb[:], in_=y_ps[s][:].rearrange("p t q -> p q t"))
-            y_bf[s] = yb
-
-        def quantize_y(s):
-            unit = max(n for n in range(len(UNITS)) if UNITS[n][0] <= s)
-            i = s - UNITS[unit][0]
+            unit, i = unit_of(s)
             if i == 0:
-                yc = work.tile([P, HALF], U32, name="yc", align_bytes=64)
-                ys = work.tile([P, HALF], U8, name="ys", align_bytes=64)
-                y_codes[unit] = yc
-                y_scales[unit] = ys
-            cols = slice(i * P, (i + 1) * P)
-            nc.vector.quantize_mx(out=y_codes[unit][:, cols].bitcast(FP8X4), scales=y_scales[unit][:, cols], in_=y_bf[s][:].rearrange("p q t -> p (q t)"))
+                yr = work.tile([P, UNIT_COLS, PACK], BF16, name="yr", bufs=2, align_bytes=64)
+                y_rows[unit] = yr
+            nc.scalar.copy(out=y_rows[unit][:, i * P : (i + 1) * P, :], in_=y_banks[s][:].rearrange("p t n -> p n t"))
+
+        def quantize_y(unit):
+            width = UNITS[unit][1] * P
+            yc = work.tile([P, UNIT_COLS], U32, name="yc", bufs=3, align_bytes=64)
+            ys = work.tile([P, UNIT_COLS], U8, name="ys", bufs=3, align_bytes=64)
+            nc.vector.quantize_mx(out=yc[:, 0:width].bitcast(FP8X4), scales=ys[:, 0:width], in_=y_rows[unit][:, 0:width, :].rearrange("p n t -> p (n t)"))
+            y_codes[unit] = yc
+            y_scales[unit] = ys
+
+        norm = {}
+        out_banks = {}
+        x_shifted = {}
+        half_done = {}
+
+        def place(unit):
+            first, count = UNITS[unit]
+            batch, row = divmod(first, ROW_BLOCKS)
+            return batch, count * P, slice(row * P, (row + count) * P)
 
         def project(unit, j):
             width = UNITS[unit][1] * P
-            o = o_pool.tile([P, HALF], F32, name="o")
+            bank = out_pool.tile([P, UNIT_COLS], F32, name="bank")
             nc.tensor.matmul_mx(
-                out=o[:, 0:width],
-                lhsT=w_codes[:, j * 2 * P : (j + 1) * 2 * P].bitcast(FP4X4),
+                out=bank[:, 0:width],
+                lhsT=w_codes[:, j * FP4_BYTES * P : (j + 1) * FP4_BYTES * P].bitcast(FP4X4),
                 lhsT_scale=w_scales[:, j * P : (j + 1) * P],
                 rhs=y_codes[unit][:, 0:width].bitcast(FP8X4),
                 rhs_scale=y_scales[unit][:, 0:width],
                 start=True,
                 stop=True,
             )
-            o_ps[unit, j] = o[:, 0:width]
+            out_banks[unit, j] = bank[:, 0:width]
 
-        def place(unit):
-            first, count = UNITS[unit]
-            b, i = divmod(first, BLOCKS)
-            return b, count * P, slice(i * P, (i + count) * P)
+        def store(unit, j, result):
+            batch, width, cols = place(unit)
+            nc.sync.dma_start(out=out[batch, j * P : (j + 1) * P, cols], in_=result)
 
-        def store(unit, j, res):
-            b, width, cols = place(unit)
-            nc.sync.dma_start(out=out[b, j * P : (j + 1) * P, cols], in_=res)
+        def shift_x(unit, j):
+            batch, width, cols = place(unit)
+            xs = work.tile([P, UNIT_COLS], F32, name="xs", bufs=8)
+            shift_col = norm["shift"][:, j : j + 1]
+            if j in SHIFT_ON_GPSIMD:
+                nc.gpsimd.tensor_scalar(out=xs[:, 0:width], in0=x_rows[batch, j][:, cols], scalar1=1.0, scalar2=shift_col, op0=MULT, op1=ADD)
+            else:
+                nc.scalar.activation(out=xs[:, 0:width], in_=x_rows[batch, j][:, cols], func=ACT.Identity, bias=shift_col)
+            x_shifted[unit, j] = xs[:, 0:width]
 
         def finish_vector(unit, j):
-            b, width, cols = place(unit)
-            rv = work.tile([P, HALF], F32, name="rv", bufs=8)
-            nc.vector.scalar_tensor_tensor(out=rv[:, 0:width], in0=o_ps[unit, j], scalar=vec["a"][:, j : j + 1], in1=x_plus[unit, j], op0=MULT, op1=ADD)
+            width = place(unit)[1]
+            rv = work.tile([P, UNIT_COLS], F32, name="rv", bufs=8)
+            nc.vector.scalar_tensor_tensor(out=rv[:, 0:width], in0=out_banks[unit, j], scalar=norm["factor"][:, j : j + 1], in1=x_shifted[unit, j], op0=MULT, op1=ADD)
             store(unit, j, rv[:, 0:width])
-
-        half_done = {}
 
         def finish_scalar(unit, j):
             width = place(unit)[1]
-            hd = work.tile([P, HALF], F32, name="hd")
-            nc.scalar.activation(out=hd[:, 0:width], in_=o_ps[unit, j], func=ACT.Identity, bias=vec["d"][:, j : j + 1], scale=vec["a"][:, j : j + 1])
+            hd = work.tile([P, UNIT_COLS], F32, name="hd")
+            nc.scalar.activation(out=hd[:, 0:width], in_=out_banks[unit, j], func=ACT.Identity, bias=norm["shift"][:, j : j + 1], scale=norm["factor"][:, j : j + 1])
             half_done[unit, j] = hd[:, 0:width]
 
         def finish_gpsimd(unit, j):
-            b, width, cols = place(unit)
-            rs = work.tile([P, HALF], F32, name="rs")
-            nc.gpsimd.tensor_tensor(out=rs[:, 0:width], in0=half_done[unit, j], in1=x_raw[b, j][:, cols], op=ADD)
-            store(unit, j, rs[:, 0:width])
+            batch, width, cols = place(unit)
+            rg = work.tile([P, UNIT_COLS], F32, name="rg")
+            nc.gpsimd.tensor_tensor(out=rg[:, 0:width], in0=half_done[unit, j], in1=x_rows[batch, j][:, cols], op=ADD)
+            store(unit, j, rg[:, 0:width])
 
-        def add_shift(unit, j):
-            b, width, cols = place(unit)
-            xp = work.tile([P, HALF], F32, name="xp", bufs=6)
-            if j in (0, 4):
-                nc.gpsimd.tensor_scalar(out=xp[:, 0:width], in0=x_raw[b, j][:, cols], scalar1=1.0, scalar2=vec["d"][:, j : j + 1], op0=MULT, op1=ADD)
-            else:
-                nc.scalar.activation(out=xp[:, 0:width], in_=x_raw[b, j][:, cols], func=ACT.Identity, bias=vec["d"][:, j : j + 1])
-            x_plus[unit, j] = xp[:, 0:width]
-
-        def group_piece(b, g, t, engine):
-            if t == 0:
-                gg = keep.tile([P, PACK * CI], BF16, name="gg_%d_%d" % (b, g), align_bytes=64)
-                g_grouped[b, g] = gg
-            src = g_raw[b, g][:].rearrange("p j (m t) -> p t m j", t=PACK)[:, t]
-            dst = g_grouped[b, g][:].rearrange("p (t m j) -> p t m j", t=PACK, j=PACK)[:, t]
-            if engine == "vector":
-                nc.vector.tensor_copy(out=dst, in_=src)
-            elif engine == "gpsimd":
-                nc.gpsimd.tensor_scalar(out=dst, in0=src, scalar1=1.0, scalar2=0.0, op0=MULT, op1=ADD)
-            else:
-                nc.scalar.copy(out=dst, in_=src)
-
-        cols5 = keep.tile([P, 5, C_BLOCKS], F32)
+        vec_f32 = keep.tile([P, P], F32)
+        vec_cols = keep.tile([P, 5, C_BLOCKS], F32)
+        bias, gamma, beta, mean, var = [vec_cols[:, v, :] for v in range(5)]
         var_eps = keep.tile([P, C_BLOCKS], F32)
         std = keep.tile([P, C_BLOCKS], F32)
-        vec_f32 = keep.tile([P, P], F32)
 
-        def vec_turn():
+        def turn_vectors():
             nc.gpsimd.tensor_copy(out=vec_f32[:], in_=vec_rows[:])
-            vec_ps = o_pool.tile([P, HALF], F32, name="o")
-            nc.tensor.transpose(vec_ps[:, 0:P], vec_f32[:], ident[:])
-            vec["ps"] = vec_ps
+            bank = out_pool.tile([P, UNIT_COLS], F32, name="bank")
+            nc.tensor.transpose(bank[:, 0:P], vec_f32[:], ident[:])
+            norm["bank"] = bank
 
-        def vec_copy():
-            nc.scalar.copy(out=cols5[:].rearrange("p v j -> p (v j)"), in_=vec["ps"][:, 0 : 5 * C_BLOCKS])
-            nc.gpsimd.tensor_scalar(out=var_eps[:], in0=cols5[:, 4, :], scalar1=1.0, scalar2=EPS, op0=MULT, op1=ADD)
-
-        def vec_sqrt():
-            nc.scalar.activation(out=std[:], in_=var_eps[:], func=ACT.Sqrt)
+        def copy_vectors():
+            nc.scalar.copy(out=vec_cols[:].rearrange("p v j -> p (v j)"), in_=norm["bank"][:, 0 : 5 * C_BLOCKS])
+            nc.gpsimd.tensor_scalar(out=var_eps[:], in0=var, scalar1=1.0, scalar2=EPS, op0=MULT, op1=ADD)
 
         def fold_norm():
             rstd = keep.tile([P, C_BLOCKS], F32, name="rstd")
             nc.vector.reciprocal(out=rstd[:], in_=std[:])
-            a = keep.tile([P, C_BLOCKS], F32, name="a")
-            nc.gpsimd.tensor_tensor(out=a[:], in0=cols5[:, 1, :], in1=rstd[:], op=MULT)
+            factor = keep.tile([P, C_BLOCKS], F32, name="factor")
+            nc.gpsimd.tensor_tensor(out=factor[:], in0=gamma, in1=rstd[:], op=MULT)
+            centred = keep.tile([P, C_BLOCKS], F32, name="centred")
+            nc.gpsimd.tensor_tensor(out=centred[:], in0=bias, in1=mean, op=SUB)
+            stretched = keep.tile([P, C_BLOCKS], F32, name="stretched")
+            nc.gpsimd.tensor_tensor(out=stretched[:], in0=centred[:], in1=factor[:], op=MULT)
             shift = keep.tile([P, C_BLOCKS], F32, name="shift")
-            nc.gpsimd.tensor_tensor(out=shift[:], in0=cols5[:, 0, :], in1=cols5[:, 3, :], op=SUB)
-            scaled = keep.tile([P, C_BLOCKS], F32, name="scaled")
-            nc.gpsimd.tensor_tensor(out=scaled[:], in0=shift[:], in1=a[:], op=MULT)
-            d = keep.tile([P, C_BLOCKS], F32, name="d")
-            nc.gpsimd.tensor_tensor(out=d[:], in0=scaled[:], in1=cols5[:, 2, :], op=ADD)
-            vec["a"] = a
-            vec["d"] = d
+            nc.gpsimd.tensor_tensor(out=shift[:], in0=stretched[:], in1=beta, op=ADD)
+            norm["factor"] = factor
+            norm["shift"] = shift
 
-        EPI = {}
-        EPI.setdefault(6, []).append((0, [0], [1]))
-        EPI.setdefault(7, []).append((0, [2], [3]))
-        EPI.setdefault(8, []).append((0, [4], [5]))
-        EPI.setdefault(9, []).append((0, [6,7], []))
-        EPI.setdefault(10, []).append((1, [0], [1]))
-        EPI.setdefault(11, []).append((1, [2], [3]))
-        EPI.setdefault(12, []).append((1, [4], [5]))
-        EPI.setdefault(13, []).append((1, [6,7], []))
-        EPI.setdefault(14, []).append((2, [0], [1]))
-        EPI.setdefault(15, []).append((2, [2], [3]))
-        EPI.setdefault(16, []).append((2, [4], [5]))
-        EPI.setdefault(16, []).append((2, [6,7], []))
-        EPI.setdefault(17, []).append((3, [0,1], [3]))
-        EPI.setdefault(17, []).append((3, [2], []))
-        EPI.setdefault(17, []).append((3, [4,5], [7]))
-        EPI.setdefault(17, []).append((3, [6], []))
-        EPI.setdefault(18, []).append((4, [0,1], [3]))
-        EPI.setdefault(18, []).append((4, [2], []))
-        EPI.setdefault(18, []).append((4, [4,5], [7]))
-        EPI.setdefault(18, []).append((4, [6], []))
-        DG = {s: ((s - 1) // 4, (s - 1) % 4) for s in range(1, 9)}
-        for s in range(3):
+        finish = {}
+        for unit in range(len(UNITS)):
+            pairs, side = (PAIRS_HALF, SCALAR_SIDE_HALF) if unit in HALF_UNITS else (PAIRS_FULL, SCALAR_SIDE_FULL)
+            for step, js in zip(FINISH_STEPS[unit], pairs):
+                finish.setdefault(step, []).append((unit, [j for j in js if j not in side], [j for j in js if j in side]))
+
+        for s in range(WIDEN_LEAD):
             widen(s)
             if s == 0:
                 turn(0)
-        group_g(0, 0, "vector")
-        for t in range(4):
-            group_piece(0, 1, t, "scalar" if t < 2 else "vector")
+        group_g(0, 0, 0, PACK, "vector")
+        group_g(0, 1, 0, PACK // 2, "scalar")
+        group_g(0, 1, PACK // 2, PACK, "vector")
         turn(1)
-        for s in range(STEPS + 6):
-            n = s - 1
-            agg = {1: [], 2: [0, 1]}.get(s, [n] if 0 <= n < STEPS else [])
-            epi = EPI.get(s, [])
-            for i in agg:
+
+        for s in range(STEPS):
+            now = finish.get(s, [])
+            ready = [s - 2, s - 1] if s % 2 == 0 and 2 <= s <= BLOCKS else []
+            for i in ready:
                 aggregate(i)
             if s == 1:
-                vec_turn()
-            if s + 2 < STEPS:
-                turn(s + 2)
-            for unit, vs, ss in epi:
-                for j in ss:
+                turn_vectors()
+            if s + TURN_LEAD < BLOCKS:
+                turn(s + TURN_LEAD)
+            for unit, on_vector, on_scalar in now:
+                for j in on_scalar:
                     finish_scalar(unit, j)
-            if s + 3 < STEPS:
-                widen(s + 3)
-            for i in agg:
+            if s + WIDEN_LEAD < BLOCKS:
+                widen(s + WIDEN_LEAD)
+            for i in ready:
                 interleave_y(i)
-            if s == 1 + 1:
-                vec_copy()
-            if s == 1 + 2:
-                vec_sqrt()
-            if s < STEPS:
+            if s == 2:
+                copy_vectors()
+            if s == 3:
+                nc.scalar.activation(out=std[:], in_=var_eps[:], func=ACT.Sqrt)
+            if s < BLOCKS:
                 scale(s)
-            if s < 2:
+            if s < PASSES:
                 quantize_g(0, s)
-            half = len(epi) // 2 if len(epi) > 1 else 0
-            flat = [(unit, j) for unit, vs, ss in epi for j in vs]
-            for unit, j in flat[: (len(flat) + 1) // 2]:
+            share = [(unit, j) for unit, on_vector, on_scalar in now for j in on_vector]
+            front = (len(share) + 1) // 2
+            for unit, j in share[:front]:
                 finish_vector(unit, j)
-            for m in {2: [], 3: [0, 1], 16: [14, 15]}.get(s, [s - 2] if 3 <= s < STEPS else []):
-                quantize_y(m)
-            if s < STEPS:
-                quantize_a(s)
-            for unit, j in flat[(len(flat) + 1) // 2 :]:
+            if s % 2 == 1 and s < BLOCKS:
+                quantize_a(s // 2)
+            for unit in range(len(UNITS)):
+                if Y_QUANTIZE_STEP[unit] == s:
+                    quantize_y(unit)
+            for unit, j in share[front:]:
                 finish_vector(unit, j)
             if s == 4:
                 fold_norm()
-            for unit, vs, ss in EPI.get(s + 1, []):
-                for j in vs:
-                    add_shift(unit, j)
-                for j in vs + ss:
+            for unit, on_vector, on_scalar in finish.get(s + SHIFT_LEAD, []):
+                for j in on_vector:
+                    shift_x(unit, j)
+            for unit, on_vector, on_scalar in finish.get(s + 1, []):
+                for j in on_vector + on_scalar:
                     project(unit, j)
-            if s in DG:
-                group_piece(1, DG[s][0], DG[s][1], "gpsimd")
-            if s in (7, 8):
-                quantize_g(1, (7, 8).index(s))
-            for unit, vs, ss in epi:
-                for j in ss:
+            if 1 <= s <= PASSES * PACK:
+                g, t = divmod(s - 1, PACK)
+                group_g(1, g, t, t + 1, "gpsimd")
+            if 8 <= s < 8 + PASSES:
+                quantize_g(1, s - 8)
+            for unit, on_vector, on_scalar in now:
+                for j in on_scalar:
                     finish_gpsimd(unit, j)

from contextlib import ExitStack

import concourse.mybir as mybir
from concourse.masks import make_identity

BATCH, C, CI, N = 2, 1024, 512, 1024
EPS = 1e-5

FLOPS = 2 * BATCH * (N * N * CI + C * CI * N)

F32 = mybir.dt.float32
BF16 = mybir.dt.bfloat16
I32 = mybir.dt.int32
U32 = mybir.dt.uint32
U8 = mybir.dt.uint8
FP8 = mybir.dt.float8_e4m3fn
FP8X4 = mybir.dt.float8_e4m3fn_x4
FP4X4 = mybir.dt.float4_e2m1fn_x4
MULT = mybir.AluOpType.mult
ADD = mybir.AluOpType.add
SUB = mybir.AluOpType.subtract
ACT = mybir.ActivationFunctionType

P = 128
PACK = 4
K_PASS = P * PACK
PASSES = N // K_PASS
ROW_BLOCKS = N // P
BLOCKS = BATCH * ROW_BLOCKS
C_BLOCKS = C // P
UNIT_COLS = 512
FP4_BYTES = 2

UNITS = ((0, 4), (4, 4), (8, 4), (12, 2), (14, 2))
HALF_UNITS = (3, 4)

WIDEN_LEAD = 3
TURN_LEAD = 2
SHIFT_LEAD = 2
Y_QUANTIZE_STEP = (5, 10, 13, 15, 17)
FINISH_STEPS = ((7, 8, 9, 10), (11, 11, 12, 13), (15, 15, 16, 16), (17, 17, 17, 17), (18, 18, 19, 19))
SCALAR_SIDE_FULL = (1, 3, 5, 7)
SCALAR_SIDE_HALF = (3, 7)
PAIRS_FULL = ((0, 1), (2, 3), (4, 5), (6, 7))
PAIRS_HALF = ((0, 1, 3), (2,), (4, 5, 7), (6,))
SHIFT_ON_GPSIMD = (0, 4)
STEPS = FINISH_STEPS[-1][-1] + 1


def tile_sgcam_pb_w4_kernel(tc, affinity_bytes, affinity_scale, g_x, w_w_words, w_w_scales, w_b, bn_gamma, bn_beta, bn_mean, bn_var, x, out):
    nc = tc.nc
    with ExitStack() as ctx:
        keep = ctx.enter_context(tc.tile_pool(name="keep", bufs=1))
        work = ctx.enter_context(tc.tile_pool(name="work", bufs=4))
        turn_pool = ctx.enter_context(tc.psum_pool(name="turn_pool", bufs=2))
        y_pool = ctx.enter_context(tc.psum_pool(name="y_pool", bufs=2))
        out_pool = ctx.enter_context(tc.psum_pool(name="out_pool", bufs=4))
        ctx.enter_context(tc.manual_schedule())

        ident = keep.tile([P, P], F32)
        make_identity(nc, ident[:])
        vec_rows = keep.tile([P, P], BF16)
        nc.vector.memset(vec_rows[:], 0.0)
        w_scales = keep.tile([P, C], U8, align_bytes=64)
        nc.vector.memset(w_scales[:].bitcast(I32), 0)
        one = keep.tile([P, 1], F32)
        nc.vector.memset(one[:], 1.0)

        k_scale = keep.tile([P, PASSES * PACK], F32)
        nc.scalar.dma_start(out=k_scale[:].rearrange("p (g t) -> p g t", t=PACK), in_=affinity_scale.rearrange("a b (g p t) -> p (a b g) t", p=P, t=PACK))
        root_of_one = keep.tile([P, 1], F32)
        nc.scalar.activation(out=root_of_one[:], in_=one[:], func=ACT.Sqrt)

        bytes_of = {}
        g_rows = {}
        x_rows = {}

        def load_bytes(first, count):
            codes_in = keep.tile([P, count, N], U8, name="codes_in_%d" % first)
            batch, row = divmod(first, ROW_BLOCKS)
            nc.sync.dma_start(out=codes_in[:], in_=affinity_bytes[batch, row * P : (row + count) * P, :].rearrange("(i p) k -> p i k", p=P))
            for i in range(count):
                bytes_of[first + i] = codes_in[:, i, :]

        def load_g(batch, g):
            rows = keep.tile([P, PACK, CI], BF16, name="g_rows_%d_%d" % (batch, g))
            nc.sync.dma_start(out=rows[:], in_=g_x[batch, g * K_PASS : (g + 1) * K_PASS, :].rearrange("(p j) n -> p j n", j=PACK))
            g_rows[batch, g] = rows

        def load_x(batch, j):
            rows = keep.tile([P, 2, N], BF16, name="x_rows_%d_%d" % (batch, j))
            nc.sync.dma_start(out=rows[:], in_=x[batch, j * P : (j + 2) * P, :].rearrange("(i p) n -> p i n", p=P))
            x_rows[batch, j] = rows[:, 0, :]
            x_rows[batch, j + 1] = rows[:, 1, :]

        load_bytes(0, 1)
        load_g(0, 0)
        load_bytes(1, 1)
        load_g(0, 1)
        load_bytes(2, 2)
        load_bytes(4, 4)
        for v, vector in enumerate((w_b, bn_gamma, bn_beta, bn_mean, bn_var)):
            nc.sync.dma_start(out=vec_rows[v * C_BLOCKS : (v + 1) * C_BLOCKS, :], in_=vector.rearrange("(j p) -> j p", p=P))
        load_g(1, 0)
        w_codes = keep.tile([P, FP4_BYTES * C], U8, align_bytes=64)
        nc.sync.dma_start(out=w_codes[:], in_=w_w_words[0])
        for q in range(4):
            nc.sync.dma_start(out=w_scales[32 * q : 32 * q + 4, :].bitcast(I32), in_=w_w_scales[0, 4 * q : 4 * q + 4, :].bitcast(I32))
        load_x(0, 0)
        load_x(0, 2)
        load_bytes(8, 4)
        load_g(1, 1)
        load_x(0, 4)
        load_x(0, 6)
        load_bytes(12, 4)
        for j in range(0, C_BLOCKS, 2):
            load_x(1, j)

        wide = {}
        turned = {}
        scaled = {}
        a_codes = {}
        a_scales = {}

        def widen(s):
            w = work.tile([P, N], BF16, name="w")
            nc.scalar.copy(out=w[:], in_=bytes_of[s].bitcast(FP8))
            wide[s] = w

        def turn(s):
            t = turn_pool.tile([P, 2 * PASSES * P], F32, name="t")
            words = wide[s][:].bitcast(F32)
            for u in range(2):
                for g in range(PASSES):
                    i = u * PASSES + g
                    nc.tensor.transpose(t[:, i * P : (i + 1) * P], words[:, 256 * g + u : 256 * (g + 1) : 2], ident[:])
            turned[s] = t

        def scale(s):
            pair, half = divmod(s, 2)
            if half == 0:
                sc = work.tile([P, 2 * N], BF16, name="sc", bufs=3, align_bytes=64)
                scaled[pair] = sc
            nc.vector.tensor_tensor(
                out=scaled[pair][:, half * N : (half + 1) * N].rearrange("p (g n u e) -> p g n u e", g=PASSES, u=2, e=2),
                in0=turned[s][:].bitcast(BF16).rearrange("p (u g n e) -> p g n u e", u=2, g=PASSES, e=2),
                in1=k_scale[:].rearrange("p (g o u e) -> p g o u e", g=PASSES, o=1, u=2, e=2).to_broadcast([P, PASSES, P, 2, 2]),
                op=MULT,
            )

        def quantize_a(pair):
            ac = work.tile([P, 2 * PASSES * P], U32, name="ac", bufs=3, align_bytes=64)
            asc = work.tile([P, 2 * PASSES * P], U8, name="asc", bufs=3, align_bytes=64)
            nc.vector.quantize_mx(out=ac[:].bitcast(FP8X4), scales=asc[:], in_=scaled[pair][:])
            a_codes[pair] = ac
            a_scales[pair] = asc

        g_grouped = {}
        g_codes = {}
        g_scales = {}

        def group_g(batch, g, first, last, engine):
            if first == 0:
                grouped = keep.tile([P, PACK * CI], BF16, name="g_grouped_%d_%d" % (batch, g), align_bytes=64)
                g_grouped[batch, g] = grouped
            src = g_rows[batch, g][:].rearrange("p j (m t) -> p t m j", t=PACK)[:, first:last]
            dst = g_grouped[batch, g][:].rearrange("p (t m j) -> p t m j", t=PACK, j=PACK)[:, first:last]
            if engine == "vector":
                nc.vector.tensor_copy(out=dst, in_=src)
            elif engine == "scalar":
                nc.scalar.copy(out=dst, in_=src)
            else:
                nc.gpsimd.tensor_scalar(out=dst, in0=src, scalar1=1.0, scalar2=0.0, op0=MULT, op1=ADD)

        def quantize_g(batch, g):
            gc = keep.tile([P, CI], U32, name="gc_%d_%d" % (batch, g), align_bytes=64)
            gs = keep.tile([P, CI], U8, name="gs_%d_%d" % (batch, g), align_bytes=64)
            nc.vector.quantize_mx(out=gc[:].bitcast(FP8X4), scales=gs[:], in_=g_grouped[batch, g][:])
            g_codes[batch, g] = gc
            g_scales[batch, g] = gs

        y_banks = {}
        y_rows = {}
        y_codes = {}
        y_scales = {}

        def unit_of(s):
            unit = max(n for n in range(len(UNITS)) if UNITS[n][0] <= s)
            return unit, s - UNITS[unit][0]

        def aggregate(s):
            batch = s // ROW_BLOCKS
            pair, half = divmod(s, 2)
            y = y_pool.tile([P, PACK, P], F32, name="y")
            for t in range(PACK):
                g_cols = slice(t * P, (t + 1) * P)
                for g in range(PASSES):
                    i = half * PASSES + g
                    a_cols = slice(i * P, (i + 1) * P)
                    nc.tensor.matmul_mx(
                        out=y[:, t, :],
                        lhsT=g_codes[batch, g][:, g_cols].bitcast(FP8X4),
                        lhsT_scale=g_scales[batch, g][:, g_cols],
                        rhs=a_codes[pair][:, a_cols].bitcast(FP8X4),
                        rhs_scale=a_scales[pair][:, a_cols],
                        start=(g == 0),
                        stop=(g == PASSES - 1),
                    )
            y_banks[s] = y

        def interleave_y(s):
            unit, i = unit_of(s)
            if i == 0:
                yr = work.tile([P, UNIT_COLS, PACK], BF16, name="yr", bufs=2, align_bytes=64)
                y_rows[unit] = yr
            nc.scalar.copy(out=y_rows[unit][:, i * P : (i + 1) * P, :], in_=y_banks[s][:].rearrange("p t n -> p n t"))

        def quantize_y(unit):
            width = UNITS[unit][1] * P
            yc = work.tile([P, UNIT_COLS], U32, name="yc", bufs=3, align_bytes=64)
            ys = work.tile([P, UNIT_COLS], U8, name="ys", bufs=3, align_bytes=64)
            nc.vector.quantize_mx(out=yc[:, 0:width].bitcast(FP8X4), scales=ys[:, 0:width], in_=y_rows[unit][:, 0:width, :].rearrange("p n t -> p (n t)"))
            y_codes[unit] = yc
            y_scales[unit] = ys

        norm = {}
        out_banks = {}
        x_shifted = {}
        half_done = {}

        def place(unit):
            first, count = UNITS[unit]
            batch, row = divmod(first, ROW_BLOCKS)
            return batch, count * P, slice(row * P, (row + count) * P)

        def project(unit, j):
            width = UNITS[unit][1] * P
            bank = out_pool.tile([P, UNIT_COLS], F32, name="bank")
            nc.tensor.matmul_mx(
                out=bank[:, 0:width],
                lhsT=w_codes[:, j * FP4_BYTES * P : (j + 1) * FP4_BYTES * P].bitcast(FP4X4),
                lhsT_scale=w_scales[:, j * P : (j + 1) * P],
                rhs=y_codes[unit][:, 0:width].bitcast(FP8X4),
                rhs_scale=y_scales[unit][:, 0:width],
                start=True,
                stop=True,
            )
            out_banks[unit, j] = bank[:, 0:width]

        def store(unit, j, result):
            batch, width, cols = place(unit)
            nc.sync.dma_start(out=out[batch, j * P : (j + 1) * P, cols], in_=result)

        def shift_x(unit, j):
            batch, width, cols = place(unit)
            xs = work.tile([P, UNIT_COLS], F32, name="xs", bufs=8)
            shift_col = norm["shift"][:, j : j + 1]
            if j in SHIFT_ON_GPSIMD:
                nc.gpsimd.tensor_scalar(out=xs[:, 0:width], in0=x_rows[batch, j][:, cols], scalar1=1.0, scalar2=shift_col, op0=MULT, op1=ADD)
            else:
                nc.scalar.activation(out=xs[:, 0:width], in_=x_rows[batch, j][:, cols], func=ACT.Identity, bias=shift_col)
            x_shifted[unit, j] = xs[:, 0:width]

        def finish_vector(unit, j):
            width = place(unit)[1]
            rv = work.tile([P, UNIT_COLS], F32, name="rv", bufs=8)
            nc.vector.scalar_tensor_tensor(out=rv[:, 0:width], in0=out_banks[unit, j], scalar=norm["factor"][:, j : j + 1], in1=x_shifted[unit, j], op0=MULT, op1=ADD)
            store(unit, j, rv[:, 0:width])

        def finish_scalar(unit, j):
            width = place(unit)[1]
            hd = work.tile([P, UNIT_COLS], F32, name="hd")
            nc.scalar.activation(out=hd[:, 0:width], in_=out_banks[unit, j], func=ACT.Identity, bias=norm["shift"][:, j : j + 1], scale=norm["factor"][:, j : j + 1])
            half_done[unit, j] = hd[:, 0:width]

        def finish_gpsimd(unit, j):
            batch, width, cols = place(unit)
            rg = work.tile([P, UNIT_COLS], F32, name="rg")
            nc.gpsimd.tensor_tensor(out=rg[:, 0:width], in0=half_done[unit, j], in1=x_rows[batch, j][:, cols], op=ADD)
            store(unit, j, rg[:, 0:width])

        vec_f32 = keep.tile([P, P], F32)
        vec_cols = keep.tile([P, 5, C_BLOCKS], F32)
        bias, gamma, beta, mean, var = [vec_cols[:, v, :] for v in range(5)]
        var_eps = keep.tile([P, C_BLOCKS], F32)
        std = keep.tile([P, C_BLOCKS], F32)

        def turn_vectors():
            nc.gpsimd.tensor_copy(out=vec_f32[:], in_=vec_rows[:])
            bank = out_pool.tile([P, UNIT_COLS], F32, name="bank")
            nc.tensor.transpose(bank[:, 0:P], vec_f32[:], ident[:])
            norm["bank"] = bank

        def copy_vectors():
            nc.scalar.copy(out=vec_cols[:].rearrange("p v j -> p (v j)"), in_=norm["bank"][:, 0 : 5 * C_BLOCKS])
            nc.gpsimd.tensor_scalar(out=var_eps[:], in0=var, scalar1=1.0, scalar2=EPS, op0=MULT, op1=ADD)

        def fold_norm():
            rstd = keep.tile([P, C_BLOCKS], F32, name="rstd")
            nc.vector.reciprocal(out=rstd[:], in_=std[:])
            factor = keep.tile([P, C_BLOCKS], F32, name="factor")
            nc.gpsimd.tensor_tensor(out=factor[:], in0=gamma, in1=rstd[:], op=MULT)
            centred = keep.tile([P, C_BLOCKS], F32, name="centred")
            nc.gpsimd.tensor_tensor(out=centred[:], in0=bias, in1=mean, op=SUB)
            stretched = keep.tile([P, C_BLOCKS], F32, name="stretched")
            nc.gpsimd.tensor_tensor(out=stretched[:], in0=centred[:], in1=factor[:], op=MULT)
            shift = keep.tile([P, C_BLOCKS], F32, name="shift")
            nc.gpsimd.tensor_tensor(out=shift[:], in0=stretched[:], in1=beta, op=ADD)
            norm["factor"] = factor
            norm["shift"] = shift

        finish = {}
        for unit in range(len(UNITS)):
            pairs, side = (PAIRS_HALF, SCALAR_SIDE_HALF) if unit in HALF_UNITS else (PAIRS_FULL, SCALAR_SIDE_FULL)
            for step, js in zip(FINISH_STEPS[unit], pairs):
                finish.setdefault(step, []).append((unit, [j for j in js if j not in side], [j for j in js if j in side]))

        for s in range(WIDEN_LEAD):
            widen(s)
            if s == 0:
                turn(0)
        group_g(0, 0, 0, PACK, "vector")
        group_g(0, 1, 0, PACK // 2, "scalar")
        group_g(0, 1, PACK // 2, PACK, "vector")
        turn(1)

        for s in range(STEPS):
            now = finish.get(s, [])
            ready = [s - 2, s - 1] if s % 2 == 0 and 2 <= s <= BLOCKS else []
            for i in ready:
                aggregate(i)
            if s == 1:
                turn_vectors()
            if s + TURN_LEAD < BLOCKS:
                turn(s + TURN_LEAD)
            for unit, on_vector, on_scalar in now:
                for j in on_scalar:
                    finish_scalar(unit, j)
            if s + WIDEN_LEAD < BLOCKS:
                widen(s + WIDEN_LEAD)
            for i in ready:
                interleave_y(i)
            if s == 2:
                copy_vectors()
            if s == 3:
                nc.scalar.activation(out=std[:], in_=var_eps[:], func=ACT.Sqrt)
            if s < BLOCKS:
                scale(s)
            if s < PASSES:
                quantize_g(0, s)
            share = [(unit, j) for unit, on_vector, on_scalar in now for j in on_vector]
            front = (len(share) + 1) // 2
            for unit, j in share[:front]:
                finish_vector(unit, j)
            if s % 2 == 1 and s < BLOCKS:
                quantize_a(s // 2)
            for unit in range(len(UNITS)):
                if Y_QUANTIZE_STEP[unit] == s:
                    quantize_y(unit)
            for unit, j in share[front:]:
                finish_vector(unit, j)
            if s == 4:
                fold_norm()
            for unit, on_vector, on_scalar in finish.get(s + SHIFT_LEAD, []):
                for j in on_vector:
                    shift_x(unit, j)
            for unit, on_vector, on_scalar in finish.get(s + 1, []):
                for j in on_vector + on_scalar:
                    project(unit, j)
            if 1 <= s <= PASSES * PACK:
                g, t = divmod(s - 1, PACK)
                group_g(1, g, t, t + 1, "gpsimd")
            if 8 <= s < 8 + PASSES:
                quantize_g(1, s - 8)
            for unit, on_vector, on_scalar in now:
                for j in on_scalar:
                    finish_gpsimd(unit, j)
